import numpy as np
import ml_dtypes


def mxq(x, axis, fmt="e4m3"):
    dtype, down = {"e4m3": (ml_dtypes.float8_e4m3fn, 7), "e5m2": (ml_dtypes.float8_e5m2, 14)}[fmt]
    v = np.moveaxis(np.asarray(x, np.float32).astype(ml_dtypes.bfloat16).astype(np.float64), axis, -1)
    blocks = v.reshape(v.shape[:-1] + (-1, 32))
    amax = np.abs(blocks).max(-1, keepdims=True)
    byte = np.maximum(np.where(amax > 0, np.frexp(amax)[1] - 1 + 127, 0) - down, 1)
    scale = np.exp2(byte - 127.0)
    codes = (blocks / scale).astype(np.float32).astype(dtype).astype(np.float64)
    return np.moveaxis((codes * scale).reshape(v.shape), -1, axis)


BF16 = ml_dtypes.bfloat16


def bf(x):
    return np.asarray(x, np.float32).astype(BF16)


def f64(x):
    return np.asarray(x).astype(np.float64)


N, T, D, E, H = 2048, 16, 64, 32, 8
ALPHA = 1.0
SIG = 2.5


def elu(x):
    return np.where(x > 0, x, ALPHA * (np.exp(x) - 1.0))


def softmax(x):
    e = np.exp(x - x.max(-1, keepdims=True))
    return e / e.sum(-1, keepdims=True)


def setup_inputs():
    return {"emb": bf(np.random.standard_normal((N, E)) * SIG / np.sqrt(E)),
            "q_proj": bf(np.random.standard_normal((N, T, D)))}


def reference(emb, q_proj):
    s = f64(emb).sum(-1)
    sim = s[:, None] - s[None, :]
    A = softmax(elu(sim)) + np.eye(N)
    y = mxq(A, 1, "e4m3") @ mxq(f64(q_proj).reshape(N, T * D), 0, "e4m3")
    return y.reshape(N, T, D).transpose(1, 0, 2)

@@ -1,0 +1,260 @@
+from contextlib import ExitStack
+
+import concourse.mybir as mybir
+from concourse.masks import make_identity
+
+F32 = mybir.dt.float32
+BF16 = mybir.dt.bfloat16
+U32 = mybir.dt.uint32
+U8 = mybir.dt.uint8
+FP8X4 = mybir.dt.float8_e4m3fn_x4
+ALU = mybir.AluOpType
+ACT = mybir.ActivationFunctionType
+AXIS = mybir.AxisListType
+
+P = 128
+NODES = 2048
+EMB = 32
+STEPS = 16
+HEAD = 64
+COLS = STEPS * HEAD
+TILES = NODES // P
+PACK = 4
+PASSES = NODES // (P * PACK)
+BANK = 512
+HALVES = COLS // BANK
+ROW_BANKS = NODES // BANK
+PER_BANK = BANK // P
+GROWTH_CAP = 80.0
+PAIR = 2
+
+FLOPS = 2 * NODES * NODES * COLS
+
+
+def tile_marketstock_crossattention_pa_kernel(tc, emb, q_proj, out):
+    nc = tc.nc
+    with ExitStack() as ctx:
+        keep = ctx.enter_context(tc.tile_pool(name="keep", bufs=1))
+        stage = ctx.enter_context(tc.tile_pool(name="stage", bufs=2))
+        rows = ctx.enter_context(tc.tile_pool(name="rows", bufs=4))
+        small = ctx.enter_context(tc.tile_pool(name="small", bufs=4))
+        resident = ctx.enter_context(tc.psum_pool(name="resident", bufs=1))
+        turned = ctx.enter_context(tc.psum_pool(name="turned", bufs=2))
+        sums = ctx.enter_context(tc.psum_pool(name="sums", bufs=2))
+        ctx.enter_context(tc.manual_schedule())
+
+        emb_sb = keep.tile([P, TILES, EMB], BF16)
+        nc.sync.dma_start(out=emb_sb[:], in_=emb.rearrange("(p i) e -> p i e", i=TILES))
+        q_raw = keep.tile([P, TILES, COLS], BF16)
+        q_rows = q_proj.rearrange("(p j) t d -> p j (t d)", j=TILES)
+        for c in range(PASSES):
+            nc.sync.dma_start(
+                out=q_raw[:, PACK * c : PACK * (c + 1), :],
+                in_=q_rows[:, PACK * c : PACK * (c + 1), :],
+            )
+
+        identity = keep.tile([P, P], F32)
+        make_identity(nc, identity[:])
+
+        warm = keep.tile([P, 1], F32)
+        nc.vector.memset(warm[:], 0.0)
+        nc.scalar.activation(out=warm[:], in_=warm[:], func=ACT.Exp)
+
+        s_col = keep.tile([P, TILES], F32)
+        nc.vector.tensor_reduce(out=s_col[:], in_=emb_sb[:], axis=AXIS.X, op=ALU.add)
+
+        s_low = keep.tile([P, 1], F32)
+        nc.vector.tensor_reduce(out=s_low[:], in_=s_col[:], axis=AXIS.X, op=ALU.min)
+        low_spread = keep.tile([P, P], F32)
+        nc.vector.tensor_copy(out=low_spread[:], in_=s_low[:].to_broadcast([P, P]))
+        low_ps = turned.tile([P, PER_BANK, P], F32, tag="turned")
+        nc.tensor.transpose(low_ps[:, 0, :], low_spread[:], identity[:])
+
+        neg_s_spread = keep.tile([P, TILES, P], F32)
+        nc.vector.tensor_scalar_mul(
+            out=neg_s_spread[:], in0=s_col[:].unsqueeze(2).to_broadcast([P, TILES, P]), scalar1=-1.0
+        )
+        neg_s_bank = []
+        for b in range(ROW_BANKS):
+            bank = resident.tile([P, PER_BANK, P], F32, name="neg_s_bank%d" % b)
+            for k in range(PER_BANK):
+                nc.tensor.transpose(bank[:, k, :], neg_s_spread[:, PER_BANK * b + k, :], identity[:])
+            neg_s_bank.append(bank)
+
+        s_min = keep.tile([P, 1], F32)
+        nc.vector.tensor_reduce(out=s_min[:], in_=low_ps[:, 0, :], axis=AXIS.X, op=ALU.min)
+
+        rise_col = keep.tile([P, TILES], F32)
+        nc.vector.tensor_scalar(
+            out=rise_col[:], in0=s_col[:], scalar1=s_min[:], scalar2=GROWTH_CAP,
+            op0=ALU.subtract, op1=ALU.min,
+        )
+        growth_col = keep.tile([P, TILES], F32)
+        nc.scalar.activation(out=growth_col[:], in_=rise_col[:], func=ACT.Exp)
+        decay_col = keep.tile([P, TILES], F32)
+        nc.scalar.activation(out=decay_col[:], in_=s_col[:], func=ACT.Exp, bias=s_min[:], scale=-1.0)
+        s_min_less_1 = keep.tile([P, 1], F32)
+        nc.vector.tensor_scalar_add(out=s_min_less_1[:], in0=s_min[:], scalar1=-1.0)
+        bias_col = keep.tile([P, TILES], F32)
+        nc.vector.tensor_scalar(
+            out=bias_col[:], in0=s_col[:], scalar1=-1.0, scalar2=s_min_less_1[:],
+            op0=ALU.mult, op1=ALU.add,
+        )
+        lift_col = keep.tile([P, TILES], F32)
+        nc.vector.tensor_scalar_add(out=lift_col[:], in0=s_col[:], scalar1=1.0)
+
+        decay_row = keep.tile([P, NODES], F32)
+        for b in range(ROW_BANKS):
+            nc.scalar.activation(
+                out=decay_row[:, BANK * b : BANK * (b + 1)],
+                in_=neg_s_bank[b][:].rearrange("p k q -> p (k q)"),
+                func=ACT.Exp, bias=s_min[:], scale=1.0,
+            )
+
+        q_codes = keep.tile([P, PASSES, COLS], U32, align_bytes=64)
+        q_scales = keep.tile([P, PASSES, COLS], U8, align_bytes=64)
+        q_grouped = {}
+
+        def regroup_q(c):
+            grouped = stage.tile([P, COLS, PACK], BF16, align_bytes=64, name="q_grouped")
+            nc.vector.tensor_copy(
+                out=grouped[:].rearrange("p (w i) t -> p w t i", i=4),
+                in_=q_raw[:, PACK * c : PACK * (c + 1), :].rearrange("p t (w i) -> p w t i", i=4),
+            )
+            q_grouped[c] = grouped
+
+        def quantise_q(c):
+            nc.vector.quantize_mx(
+                out=q_codes[:, c, :].bitcast(FP8X4),
+                scales=q_scales[:, c, :],
+                in_=q_grouped[c][:].rearrange("p w t -> p (w t)"),
+            )
+
+        for c in range(PASSES + 1):
+            if c < PASSES:
+                regroup_q(c)
+            if c > 0:
+                quantise_q(c - 1)
+
+        e_rows = {}
+        row_sums = {}
+        inv_sums = {}
+        a_rows = {}
+        a_grouped = {}
+        a_codes = {}
+        a_scales = {}
+        o_tiles = {}
+        out_rows = out.rearrange("t (p i) d -> p t i d", i=TILES)
+
+        def capped_exp(i):
+            e_row = rows.tile([P, NODES], F32, name="e_row")
+            nc.vector.tensor_scalar(
+                out=e_row[:], in0=decay_row[:],
+                scalar1=decay_col[:, i : i + 1], scalar2=growth_col[:, i : i + 1],
+                op0=ALU.min, op1=ALU.mult,
+            )
+            e_rows[i] = e_row
+
+        def elu_plus_1(i):
+            e_row = e_rows[i]
+            for b in range(ROW_BANKS):
+                piece = e_row[:, BANK * b : BANK * (b + 1)]
+                nc.vector.scalar_tensor_tensor(
+                    out=piece, in0=neg_s_bank[b][:].rearrange("p k q -> p (k q)"),
+                    scalar=lift_col[:, i : i + 1], in1=piece, op0=ALU.add, op1=ALU.max,
+                )
+
+        def numerators(i):
+            row_sum = small.tile([P, 1], F32, name="row_sum")
+            nc.scalar.activation(
+                out=e_rows[i][:], in_=e_rows[i][:], func=ACT.Exp,
+                bias=bias_col[:, i : i + 1], scale=1.0, accum_out=row_sum[:],
+            )
+            row_sums[i] = row_sum
+
+        def add_identity(i):
+            e_row = e_rows[i]
+            row_sum = row_sums[i]
+            own = e_row[:, P * i : P * (i + 1)]
+            nc.vector.scalar_tensor_tensor(
+                out=own, in0=identity[:], scalar=row_sum[:], in1=own, op0=ALU.mult, op1=ALU.add,
+            )
+            inv_sum = small.tile([P, 1], F32, name="inv_sum")
+            nc.vector.reciprocal(out=inv_sum[:], in_=row_sum[:])
+            inv_sums[i] = inv_sum
+
+        def normalise(i):
+            a_row = stage.tile([P, NODES], BF16, name="a_row")
+            nc.gpsimd.tensor_scalar(
+                out=a_row[:].rearrange("p (k q e) -> p k q e", q=P, e=2),
+                in0=e_rows[i][:].rearrange("p (k e q) -> p k q e", q=P, e=2),
+                scalar1=inv_sums[i][:], scalar2=0.0, op0=ALU.mult, op1=ALU.add,
+            )
+            a_rows[i] = a_row
+
+        def turn(i):
+            words = a_rows[i][:].bitcast(F32)
+            grouped = stage.tile([P, NODES], BF16, align_bytes=64, name="a_grouped")
+            grouped_words = grouped[:].bitcast(F32).rearrange("p (c n u) -> p c n u", n=P, u=2)
+            for b in range(HALVES):
+                a_ps = turned.tile([P, PER_BANK, P], F32, tag="turned")
+                for k in range(PER_BANK):
+                    block = PER_BANK * b + k
+                    nc.tensor.transpose(a_ps[:, k, :], words[:, P * block : P * (block + 1)], identity[:])
+                nc.scalar.copy(
+                    out=grouped_words[:, 2 * b : 2 * (b + 1), :, :],
+                    in_=a_ps[:].rearrange("p (c u) n -> p c n u", u=2),
+                )
+            a_grouped[i] = grouped
+
+        def quantise(i):
+            codes = stage.tile([P, PASSES * P], U32, align_bytes=64, name="a_codes")
+            scales = stage.tile([P, PASSES * P], U8, align_bytes=64, name="a_scales")
+            nc.vector.quantize_mx(out=codes[:].bitcast(FP8X4), scales=scales[:], in_=a_grouped[i][:])
+            a_codes[i] = codes
+            a_scales[i] = scales
+
+        def multiply_and_store(i):
+            pair, member = divmod(i, PAIR)
+            if member == 0:
+                o_tiles[pair] = stage.tile([P, STEPS, PAIR, HEAD], F32, name="o_tile")
+            o_tile = o_tiles[pair]
+            steps = STEPS // HALVES
+            for h in range(HALVES):
+                acc = sums.tile([P, BANK], F32, name="acc")
+                for c in range(PASSES):
+                    nc.tensor.matmul_mx(
+                        out=acc[:],
+                        lhsT=a_codes[i][:, P * c : P * (c + 1)].bitcast(FP8X4),
+                        lhsT_scale=a_scales[i][:, P * c : P * (c + 1)],
+                        rhs=q_codes[:, c, BANK * h : BANK * (h + 1)].bitcast(FP8X4),
+                        rhs_scale=q_scales[:, c, BANK * h : BANK * (h + 1)],
+                        start=(c == 0),
+                        stop=(c == PASSES - 1),
+                    )
+                nc.scalar.copy(
+                    out=o_tile[:, steps * h : steps * (h + 1), member, :],
+                    in_=acc[:].rearrange("p (t d) -> p t d", d=HEAD),
+                )
+            if member == PAIR - 1:
+                nc.sync.dma_start(
+                    out=out_rows[:, :, PAIR * pair : PAIR * (pair + 1), :], in_=o_tile[:]
+                )
+
+        capped_exp(0)
+        for step in range(TILES + 4):
+            if 0 <= step - 2 < TILES:
+                add_identity(step - 2)
+                normalise(step - 2)
+            if step < TILES:
+                elu_plus_1(step)
+            if 0 <= step - 3 < TILES:
+                turn(step - 3)
+            if 0 <= step - 4 < TILES:
+                multiply_and_store(step - 4)
+            if step < TILES:
+                numerators(step)
+            if 0 <= step - 3 < TILES:
+                quantise(step - 3)
+            if step + 1 < TILES:
+                capped_exp(step + 1)

@@ -27,6 +27,7 @@ ROW_BANKS = NODES // BANK
 PER_BANK = BANK // P
 GROWTH_CAP = 80.0
 PAIR = 2
+VECTOR_PASSES = 2
 
 FLOPS = 2 * NODES * NODES * COLS
 
@@ -70,9 +71,11 @@ def tile_marketstock_crossattention_pa_kernel(tc, emb, q_proj, out):
         low_ps = turned.tile([P, PER_BANK, P], F32, tag="turned")
         nc.tensor.transpose(low_ps[:, 0, :], low_spread[:], identity[:])
 
+        neg_s_col = keep.tile([P, TILES], F32)
+        nc.vector.tensor_scalar_mul(out=neg_s_col[:], in0=s_col[:], scalar1=-1.0)
         neg_s_spread = keep.tile([P, TILES, P], F32)
-        nc.vector.tensor_scalar_mul(
-            out=neg_s_spread[:], in0=s_col[:].unsqueeze(2).to_broadcast([P, TILES, P]), scalar1=-1.0
+        nc.vector.tensor_copy(
+            out=neg_s_spread[:], in_=neg_s_col[:].unsqueeze(2).to_broadcast([P, TILES, P])
         )
         neg_s_bank = []
         for b in range(ROW_BANKS):
@@ -91,17 +94,8 @@ def tile_marketstock_crossattention_pa_kernel(tc, emb, q_proj, out):
         )
         growth_col = keep.tile([P, TILES], F32)
         nc.scalar.activation(out=growth_col[:], in_=rise_col[:], func=ACT.Exp)
-        decay_col = keep.tile([P, TILES], F32)
-        nc.scalar.activation(out=decay_col[:], in_=s_col[:], func=ACT.Exp, bias=s_min[:], scale=-1.0)
-        s_min_less_1 = keep.tile([P, 1], F32)
-        nc.vector.tensor_scalar_add(out=s_min_less_1[:], in0=s_min[:], scalar1=-1.0)
-        bias_col = keep.tile([P, TILES], F32)
-        nc.vector.tensor_scalar(
-            out=bias_col[:], in0=s_col[:], scalar1=-1.0, scalar2=s_min_less_1[:],
-            op0=ALU.mult, op1=ALU.add,
-        )
-        lift_col = keep.tile([P, TILES], F32)
-        nc.vector.tensor_scalar_add(out=lift_col[:], in0=s_col[:], scalar1=1.0)
+        drop_col = keep.tile([P, TILES], F32)
+        nc.vector.tensor_scalar_add(out=drop_col[:], in0=neg_s_col[:], scalar1=-1.0)
 
         decay_row = keep.tile([P, NODES], F32)
         for b in range(ROW_BANKS):
@@ -111,34 +105,8 @@ def tile_marketstock_crossattention_pa_kernel(tc, emb, q_proj, out):
                 func=ACT.Exp, bias=s_min[:], scale=1.0,
             )
 
-        q_codes = keep.tile([P, PASSES, COLS], U32, align_bytes=64)
-        q_scales = keep.tile([P, PASSES, COLS], U8, align_bytes=64)
-        q_grouped = {}
-
-        def regroup_q(c):
-            grouped = stage.tile([P, COLS, PACK], BF16, align_bytes=64, name="q_grouped")
-            nc.vector.tensor_copy(
-                out=grouped[:].rearrange("p (w i) t -> p w t i", i=4),
-                in_=q_raw[:, PACK * c : PACK * (c + 1), :].rearrange("p t (w i) -> p w t i", i=4),
-            )
-            q_grouped[c] = grouped
-
-        def quantise_q(c):
-            nc.vector.quantize_mx(
-                out=q_codes[:, c, :].bitcast(FP8X4),
-                scales=q_scales[:, c, :],
-                in_=q_grouped[c][:].rearrange("p w t -> p (w t)"),
-            )
-
-        for c in range(PASSES + 1):
-            if c < PASSES:
-                regroup_q(c)
-            if c > 0:
-                quantise_q(c - 1)
-
         e_rows = {}
         row_sums = {}
-        inv_sums = {}
         a_rows = {}
         a_grouped = {}
         a_codes = {}
@@ -146,33 +114,33 @@ def tile_marketstock_crossattention_pa_kernel(tc, emb, q_proj, out):
         o_tiles = {}
         out_rows = out.rearrange("t (p i) d -> p t i d", i=TILES)
 
-        def capped_exp(i):
+        def exp_x_shifted(i):
             e_row = rows.tile([P, NODES], F32, name="e_row")
-            nc.vector.tensor_scalar(
+            nc.gpsimd.tensor_scalar(
                 out=e_row[:], in0=decay_row[:],
-                scalar1=decay_col[:, i : i + 1], scalar2=growth_col[:, i : i + 1],
-                op0=ALU.min, op1=ALU.mult,
+                scalar1=growth_col[:, i : i + 1], scalar2=drop_col[:, i : i + 1],
+                op0=ALU.mult, op1=ALU.add,
             )
             e_rows[i] = e_row
 
-        def elu_plus_1(i):
+        def elu_shifted(i):
             e_row = e_rows[i]
             for b in range(ROW_BANKS):
                 piece = e_row[:, BANK * b : BANK * (b + 1)]
                 nc.vector.scalar_tensor_tensor(
-                    out=piece, in0=neg_s_bank[b][:].rearrange("p k q -> p (k q)"),
-                    scalar=lift_col[:, i : i + 1], in1=piece, op0=ALU.add, op1=ALU.max,
+                    out=piece, in0=piece, scalar=neg_s_col[:, i : i + 1],
+                    in1=neg_s_bank[b][:].rearrange("p k q -> p (k q)"), op0=ALU.min, op1=ALU.max,
                 )
 
         def numerators(i):
             row_sum = small.tile([P, 1], F32, name="row_sum")
             nc.scalar.activation(
                 out=e_rows[i][:], in_=e_rows[i][:], func=ACT.Exp,
-                bias=bias_col[:, i : i + 1], scale=1.0, accum_out=row_sum[:],
+                bias=s_min[:], scale=1.0, accum_out=row_sum[:],
             )
             row_sums[i] = row_sum
 
-        def add_identity(i):
+        def adjacency(i):
             e_row = e_rows[i]
             row_sum = row_sums[i]
             own = e_row[:, P * i : P * (i + 1)]
@@ -181,14 +149,11 @@ def tile_marketstock_crossattention_pa_kernel(tc, emb, q_proj, out):
             )
             inv_sum = small.tile([P, 1], F32, name="inv_sum")
             nc.vector.reciprocal(out=inv_sum[:], in_=row_sum[:])
-            inv_sums[i] = inv_sum
-
-        def normalise(i):
             a_row = stage.tile([P, NODES], BF16, name="a_row")
-            nc.gpsimd.tensor_scalar(
+            nc.vector.tensor_scalar_mul(
                 out=a_row[:].rearrange("p (k q e) -> p k q e", q=P, e=2),
-                in0=e_rows[i][:].rearrange("p (k e q) -> p k q e", q=P, e=2),
-                scalar1=inv_sums[i][:], scalar2=0.0, op0=ALU.mult, op1=ALU.add,
+                in0=e_row[:].rearrange("p (k e q) -> p k q e", q=P, e=2),
+                scalar1=inv_sum[:],
             )
             a_rows[i] = a_row
 
@@ -219,8 +184,8 @@ def tile_marketstock_crossattention_pa_kernel(tc, emb, q_proj, out):
             if member == 0:
                 o_tiles[pair] = stage.tile([P, STEPS, PAIR, HEAD], F32, name="o_tile")
             o_tile = o_tiles[pair]
-            steps = STEPS // HALVES
             for h in range(HALVES):
+                steps = slice(STEPS // HALVES * h, STEPS // HALVES * (h + 1))
                 acc = sums.tile([P, BANK], F32, name="acc")
                 for c in range(PASSES):
                     nc.tensor.matmul_mx(
@@ -233,28 +198,55 @@ def tile_marketstock_crossattention_pa_kernel(tc, emb, q_proj, out):
                         stop=(c == PASSES - 1),
                     )
                 nc.scalar.copy(
-                    out=o_tile[:, steps * h : steps * (h + 1), member, :],
-                    in_=acc[:].rearrange("p (t d) -> p t d", d=HEAD),
+                    out=o_tile[:, steps, member, :], in_=acc[:].rearrange("p (t d) -> p t d", d=HEAD)
                 )
-            if member == PAIR - 1:
-                nc.sync.dma_start(
-                    out=out_rows[:, :, PAIR * pair : PAIR * (pair + 1), :], in_=o_tile[:]
-                )
+                if member == PAIR - 1:
+                    nc.sync.dma_start(
+                        out=out_rows[:, steps, PAIR * pair : PAIR * (pair + 1), :],
+                        in_=o_tile[:, steps, :, :],
+                    )
 
-        capped_exp(0)
-        for step in range(TILES + 4):
-            if 0 <= step - 2 < TILES:
-                add_identity(step - 2)
-                normalise(step - 2)
+        q_codes = keep.tile([P, PASSES, COLS], U32, align_bytes=64)
+        q_scales = keep.tile([P, PASSES, COLS], U8, align_bytes=64)
+        q_grouped = {}
+
+        def regroup_q(c):
+            grouped = keep.tile([P, COLS, PACK], BF16, align_bytes=64, name="q_grouped%d" % c)
+            copy = nc.vector.tensor_copy if c < VECTOR_PASSES else nc.scalar.copy
+            copy(
+                out=grouped[:].rearrange("p (w i) t -> p w t i", i=4),
+                in_=q_raw[:, PACK * c : PACK * (c + 1), :].rearrange("p t (w i) -> p w t i", i=4),
+            )
+            q_grouped[c] = grouped
+
+        def quantise_q(c):
+            nc.vector.quantize_mx(
+                out=q_codes[:, c, :].bitcast(FP8X4),
+                scales=q_scales[:, c, :],
+                in_=q_grouped[c][:].rearrange("p w t -> p (w t)"),
+            )
+
+        exp_x_shifted(0)
+        exp_x_shifted(1)
+        for c in range(PASSES):
+            regroup_q(c)
+        for c in range(VECTOR_PASSES):
+            quantise_q(c)
+
+        for step in range(TILES + 3):
             if step < TILES:
-                elu_plus_1(step)
+                elu_shifted(step)
+            if step + 2 < TILES:
+                exp_x_shifted(step + 2)
+            if 0 <= step - 2 < TILES:
+                turn(step - 2)
             if 0 <= step - 3 < TILES:
-                turn(step - 3)
-            if 0 <= step - 4 < TILES:
-                multiply_and_store(step - 4)
+                multiply_and_store(step - 3)
             if step < TILES:
                 numerators(step)
-            if 0 <= step - 3 < TILES:
-                quantise(step - 3)
-            if step + 1 < TILES:
-                capped_exp(step + 1)
+            if 0 <= step - 1 < TILES:
+                adjacency(step - 1)
+            if 0 <= step - 2 < TILES:
+                quantise(step - 2)
+            if VECTOR_PASSES + step < PASSES:
+                quantise_q(VECTOR_PASSES + step)

@@ -27,7 +27,7 @@ ROW_BANKS = NODES // BANK
 PER_BANK = BANK // P
 GROWTH_CAP = 80.0
 PAIR = 2
-VECTOR_PASSES = 2
+VECTOR_PASSES = 3
 
 FLOPS = 2 * NODES * NODES * COLS
 
@@ -114,9 +114,9 @@ def tile_marketstock_crossattention_pa_kernel(tc, emb, q_proj, out):
         o_tiles = {}
         out_rows = out.rearrange("t (p i) d -> p t i d", i=TILES)
 
-        def exp_x_shifted(i):
+        def exp_x_shifted(i, engine):
             e_row = rows.tile([P, NODES], F32, name="e_row")
-            nc.gpsimd.tensor_scalar(
+            engine.tensor_scalar(
                 out=e_row[:], in0=decay_row[:],
                 scalar1=growth_col[:, i : i + 1], scalar2=drop_col[:, i : i + 1],
                 op0=ALU.mult, op1=ALU.add,
@@ -226,18 +226,18 @@ def tile_marketstock_crossattention_pa_kernel(tc, emb, q_proj, out):
                 in_=q_grouped[c][:].rearrange("p w t -> p (w t)"),
             )
 
-        exp_x_shifted(0)
-        exp_x_shifted(1)
         for c in range(PASSES):
             regroup_q(c)
         for c in range(VECTOR_PASSES):
             quantise_q(c)
 
+        exp_x_shifted(0, nc.vector)
+
         for step in range(TILES + 3):
             if step < TILES:
                 elu_shifted(step)
-            if step + 2 < TILES:
-                exp_x_shifted(step + 2)
+            if step + 1 < TILES:
+                exp_x_shifted(step + 1, nc.gpsimd)
             if 0 <= step - 2 < TILES:
                 turn(step - 2)
             if 0 <= step - 3 < TILES:

from contextlib import ExitStack

import concourse.mybir as mybir
from concourse.masks import make_identity

F32 = mybir.dt.float32
BF16 = mybir.dt.bfloat16
U32 = mybir.dt.uint32
U8 = mybir.dt.uint8
FP8X4 = mybir.dt.float8_e4m3fn_x4
ALU = mybir.AluOpType
ACT = mybir.ActivationFunctionType
AXIS = mybir.AxisListType

P = 128
NODES = 2048
EMB = 32
STEPS = 16
HEAD = 64
COLS = STEPS * HEAD
TILES = NODES // P
PACK = 4
PASSES = NODES // (P * PACK)
BANK = 512
HALVES = COLS // BANK
ROW_BANKS = NODES // BANK
PER_BANK = BANK // P
GROWTH_CAP = 80.0
PAIR = 2
VECTOR_PASSES = 3

FLOPS = 2 * NODES * NODES * COLS


def tile_marketstock_crossattention_pa_kernel(tc, emb, q_proj, out):
    nc = tc.nc
    with ExitStack() as ctx:
        keep = ctx.enter_context(tc.tile_pool(name="keep", bufs=1))
        stage = ctx.enter_context(tc.tile_pool(name="stage", bufs=2))
        rows = ctx.enter_context(tc.tile_pool(name="rows", bufs=4))
        small = ctx.enter_context(tc.tile_pool(name="small", bufs=4))
        resident = ctx.enter_context(tc.psum_pool(name="resident", bufs=1))
        turned = ctx.enter_context(tc.psum_pool(name="turned", bufs=2))
        sums = ctx.enter_context(tc.psum_pool(name="sums", bufs=2))
        ctx.enter_context(tc.manual_schedule())

        emb_sb = keep.tile([P, TILES, EMB], BF16)
        nc.sync.dma_start(out=emb_sb[:], in_=emb.rearrange("(p i) e -> p i e", i=TILES))
        q_raw = keep.tile([P, TILES, COLS], BF16)
        q_rows = q_proj.rearrange("(p j) t d -> p j (t d)", j=TILES)
        for c in range(PASSES):
            nc.sync.dma_start(
                out=q_raw[:, PACK * c : PACK * (c + 1), :],
                in_=q_rows[:, PACK * c : PACK * (c + 1), :],
            )

        identity = keep.tile([P, P], F32)
        make_identity(nc, identity[:])

        warm = keep.tile([P, 1], F32)
        nc.vector.memset(warm[:], 0.0)
        nc.scalar.activation(out=warm[:], in_=warm[:], func=ACT.Exp)

        s_col = keep.tile([P, TILES], F32)
        nc.vector.tensor_reduce(out=s_col[:], in_=emb_sb[:], axis=AXIS.X, op=ALU.add)

        s_low = keep.tile([P, 1], F32)
        nc.vector.tensor_reduce(out=s_low[:], in_=s_col[:], axis=AXIS.X, op=ALU.min)
        low_spread = keep.tile([P, P], F32)
        nc.vector.tensor_copy(out=low_spread[:], in_=s_low[:].to_broadcast([P, P]))
        low_ps = turned.tile([P, PER_BANK, P], F32, tag="turned")
        nc.tensor.transpose(low_ps[:, 0, :], low_spread[:], identity[:])

        neg_s_col = keep.tile([P, TILES], F32)
        nc.vector.tensor_scalar_mul(out=neg_s_col[:], in0=s_col[:], scalar1=-1.0)
        neg_s_spread = keep.tile([P, TILES, P], F32)
        nc.vector.tensor_copy(
            out=neg_s_spread[:], in_=neg_s_col[:].unsqueeze(2).to_broadcast([P, TILES, P])
        )
        neg_s_bank = []
        for b in range(ROW_BANKS):
            bank = resident.tile([P, PER_BANK, P], F32, name="neg_s_bank%d" % b)
            for k in range(PER_BANK):
                nc.tensor.transpose(bank[:, k, :], neg_s_spread[:, PER_BANK * b + k, :], identity[:])
            neg_s_bank.append(bank)

        s_min = keep.tile([P, 1], F32)
        nc.vector.tensor_reduce(out=s_min[:], in_=low_ps[:, 0, :], axis=AXIS.X, op=ALU.min)

        rise_col = keep.tile([P, TILES], F32)
        nc.vector.tensor_scalar(
            out=rise_col[:], in0=s_col[:], scalar1=s_min[:], scalar2=GROWTH_CAP,
            op0=ALU.subtract, op1=ALU.min,
        )
        growth_col = keep.tile([P, TILES], F32)
        nc.scalar.activation(out=growth_col[:], in_=rise_col[:], func=ACT.Exp)
        drop_col = keep.tile([P, TILES], F32)
        nc.vector.tensor_scalar_add(out=drop_col[:], in0=neg_s_col[:], scalar1=-1.0)

        decay_row = keep.tile([P, NODES], F32)
        for b in range(ROW_BANKS):
            nc.scalar.activation(
                out=decay_row[:, BANK * b : BANK * (b + 1)],
                in_=neg_s_bank[b][:].rearrange("p k q -> p (k q)"),
                func=ACT.Exp, bias=s_min[:], scale=1.0,
            )

        e_rows = {}
        row_sums = {}
        a_rows = {}
        a_grouped = {}
        a_codes = {}
        a_scales = {}
        o_tiles = {}
        out_rows = out.rearrange("t (p i) d -> p t i d", i=TILES)

        def exp_x_shifted(i, engine):
            e_row = rows.tile([P, NODES], F32, name="e_row")
            engine.tensor_scalar(
                out=e_row[:], in0=decay_row[:],
                scalar1=growth_col[:, i : i + 1], scalar2=drop_col[:, i : i + 1],
                op0=ALU.mult, op1=ALU.add,
            )
            e_rows[i] = e_row

        def elu_shifted(i):
            e_row = e_rows[i]
            for b in range(ROW_BANKS):
                piece = e_row[:, BANK * b : BANK * (b + 1)]
                nc.vector.scalar_tensor_tensor(
                    out=piece, in0=piece, scalar=neg_s_col[:, i : i + 1],
                    in1=neg_s_bank[b][:].rearrange("p k q -> p (k q)"), op0=ALU.min, op1=ALU.max,
                )

        def numerators(i):
            row_sum = small.tile([P, 1], F32, name="row_sum")
            nc.scalar.activation(
                out=e_rows[i][:], in_=e_rows[i][:], func=ACT.Exp,
                bias=s_min[:], scale=1.0, accum_out=row_sum[:],
            )
            row_sums[i] = row_sum

        def adjacency(i):
            e_row = e_rows[i]
            row_sum = row_sums[i]
            own = e_row[:, P * i : P * (i + 1)]
            nc.vector.scalar_tensor_tensor(
                out=own, in0=identity[:], scalar=row_sum[:], in1=own, op0=ALU.mult, op1=ALU.add,
            )
            inv_sum = small.tile([P, 1], F32, name="inv_sum")
            nc.vector.reciprocal(out=inv_sum[:], in_=row_sum[:])
            a_row = stage.tile([P, NODES], BF16, name="a_row")
            nc.vector.tensor_scalar_mul(
                out=a_row[:].rearrange("p (k q e) -> p k q e", q=P, e=2),
                in0=e_row[:].rearrange("p (k e q) -> p k q e", q=P, e=2),
                scalar1=inv_sum[:],
            )
            a_rows[i] = a_row

        def turn(i):
            words = a_rows[i][:].bitcast(F32)
            grouped = stage.tile([P, NODES], BF16, align_bytes=64, name="a_grouped")
            grouped_words = grouped[:].bitcast(F32).rearrange("p (c n u) -> p c n u", n=P, u=2)
            for b in range(HALVES):
                a_ps = turned.tile([P, PER_BANK, P], F32, tag="turned")
                for k in range(PER_BANK):
                    block = PER_BANK * b + k
                    nc.tensor.transpose(a_ps[:, k, :], words[:, P * block : P * (block + 1)], identity[:])
                nc.scalar.copy(
                    out=grouped_words[:, 2 * b : 2 * (b + 1), :, :],
                    in_=a_ps[:].rearrange("p (c u) n -> p c n u", u=2),
                )
            a_grouped[i] = grouped

        def quantise(i):
            codes = stage.tile([P, PASSES * P], U32, align_bytes=64, name="a_codes")
            scales = stage.tile([P, PASSES * P], U8, align_bytes=64, name="a_scales")
            nc.vector.quantize_mx(out=codes[:].bitcast(FP8X4), scales=scales[:], in_=a_grouped[i][:])
            a_codes[i] = codes
            a_scales[i] = scales

        def multiply_and_store(i):
            pair, member = divmod(i, PAIR)
            if member == 0:
                o_tiles[pair] = stage.tile([P, STEPS, PAIR, HEAD], F32, name="o_tile")
            o_tile = o_tiles[pair]
            for h in range(HALVES):
                steps = slice(STEPS // HALVES * h, STEPS // HALVES * (h + 1))
                acc = sums.tile([P, BANK], F32, name="acc")
                for c in range(PASSES):
                    nc.tensor.matmul_mx(
                        out=acc[:],
                        lhsT=a_codes[i][:, P * c : P * (c + 1)].bitcast(FP8X4),
                        lhsT_scale=a_scales[i][:, P * c : P * (c + 1)],
                        rhs=q_codes[:, c, BANK * h : BANK * (h + 1)].bitcast(FP8X4),
                        rhs_scale=q_scales[:, c, BANK * h : BANK * (h + 1)],
                        start=(c == 0),
                        stop=(c == PASSES - 1),
                    )
                nc.scalar.copy(
                    out=o_tile[:, steps, member, :], in_=acc[:].rearrange("p (t d) -> p t d", d=HEAD)
                )
                if member == PAIR - 1:
                    nc.sync.dma_start(
                        out=out_rows[:, steps, PAIR * pair : PAIR * (pair + 1), :],
                        in_=o_tile[:, steps, :, :],
                    )

        q_codes = keep.tile([P, PASSES, COLS], U32, align_bytes=64)
        q_scales = keep.tile([P, PASSES, COLS], U8, align_bytes=64)
        q_grouped = {}

        def regroup_q(c):
            grouped = keep.tile([P, COLS, PACK], BF16, align_bytes=64, name="q_grouped%d" % c)
            copy = nc.vector.tensor_copy if c < VECTOR_PASSES else nc.scalar.copy
            copy(
                out=grouped[:].rearrange("p (w i) t -> p w t i", i=4),
                in_=q_raw[:, PACK * c : PACK * (c + 1), :].rearrange("p t (w i) -> p w t i", i=4),
            )
            q_grouped[c] = grouped

        def quantise_q(c):
            nc.vector.quantize_mx(
                out=q_codes[:, c, :].bitcast(FP8X4),
                scales=q_scales[:, c, :],
                in_=q_grouped[c][:].rearrange("p w t -> p (w t)"),
            )

        for c in range(PASSES):
            regroup_q(c)
        for c in range(VECTOR_PASSES):
            quantise_q(c)

        exp_x_shifted(0, nc.vector)

        for step in range(TILES + 3):
            if step < TILES:
                elu_shifted(step)
            if step + 1 < TILES:
                exp_x_shifted(step + 1, nc.gpsimd)
            if 0 <= step - 2 < TILES:
                turn(step - 2)
            if 0 <= step - 3 < TILES:
                multiply_and_store(step - 3)
            if step < TILES:
                numerators(step)
            if 0 <= step - 1 < TILES:
                adjacency(step - 1)
            if 0 <= step - 2 < TILES:
                quantise(step - 2)
            if VECTOR_PASSES + step < PASSES:
                quantise_q(VECTOR_PASSES + step)
